import numpy as np
import ml_dtypes


def mxq(x, axis, fmt="e4m3"):
    dtype, down = {"e4m3": (ml_dtypes.float8_e4m3fn, 7), "e5m2": (ml_dtypes.float8_e5m2, 14)}[fmt]
    v = np.moveaxis(np.asarray(x, np.float32).astype(ml_dtypes.bfloat16).astype(np.float64), axis, -1)
    blocks = v.reshape(v.shape[:-1] + (-1, 32))
    amax = np.abs(blocks).max(-1, keepdims=True)
    byte = np.maximum(np.where(amax > 0, np.frexp(amax)[1] - 1 + 127, 0) - down, 1)
    scale = np.exp2(byte - 127.0)
    codes = (blocks / scale).astype(np.float32).astype(dtype).astype(np.float64)
    return np.moveaxis((codes * scale).reshape(v.shape), -1, axis)


WIDE = False


def mx_kscale(k):
    if not WIDE:
        return np.ones(k)
    levels = np.array([10, -10, 5, -5, 0])
    if k % 512:
        return np.exp2(np.random.permutation(np.resize(levels, k // 32))).repeat(32)
    a = np.empty((k // 512, 16))
    for p in range(k // 512):
        a[p, :8] = np.random.permutation(np.resize(levels, 8))
        for g in range(8):
            far = levels[np.abs(levels - a[p, g]) >= 10]
            a[p, g + 8] = far[np.random.randint(len(far))]
    return np.exp2(a.ravel()).repeat(32)


BF16 = ml_dtypes.bfloat16


def bf(x):
    return np.asarray(x, np.float32).astype(BF16)


def f64(x):
    return np.asarray(x).astype(np.float64)


B, N, K, H, C_E, M = 2, 64, 16, 1024, 1024, 1024
SCALE = 30.0


def draw0():
    s = mx_kscale(M)
    return {"h2": bf(np.random.standard_normal((B, N, K, M)) * 0.65 * s),
            "h_V": bf(np.random.standard_normal((B, N, H))),
            "mask_attend": bf(np.random.uniform(size=(B, N, K)) < 0.9),
            "W3_w": bf(np.random.standard_normal((M, H)) * 4.0 / np.sqrt(M) / s[:, None]),
            "W3_b": bf(np.random.standard_normal(H) * 0.1)}


def core(h2, h_V, mask_attend, W3_w, W3_b):
    h_message = (mxq(f64(h2), 3, "e4m3") @ mxq(f64(W3_w), 0, "e4m3")) + f64(W3_b)
    h_message = f64(mask_attend)[..., None] * h_message
    dh = np.sum(h_message, axis=-2) / SCALE
    return f64(h_V) + dh


def e4m3fn_bytes(y):
    return np.clip(np.asarray(y, np.float64), -448.0, 448.0).astype(np.float32).astype(ml_dtypes.float8_e4m3fn).view(np.uint8)


def e4m3fn_values(b):
    return np.asarray(b, np.uint8).view(ml_dtypes.float8_e4m3fn).astype(np.float64)


def setup_inputs():
    d = draw0()
    x0 = np.asarray(d['h2']).astype(np.float64)
    s = (np.max(np.abs(x0), axis=(0, 1, 2), keepdims=True) / 448.0).astype(np.float32)
    out = {}
    for k, v in d.items():
        if k == 'h2':
            out['h2_bytes'] = e4m3fn_bytes(x0 / s.astype(np.float64))
            out['h2_scale'] = s
        else:
            out[k] = v
    return out


def reference(h2_bytes, h2_scale, h_V, mask_attend, W3_w, W3_b):
    return core(e4m3fn_values(h2_bytes) * h2_scale.astype(np.float64), h_V, mask_attend, W3_w, W3_b)

@@ -1,0 +1,283 @@
+from contextlib import ExitStack
+
+import concourse.mybir as mybir
+from concourse.masks import make_identity
+
+FLOPS = 2 * 2048 * 1024 * 1024
+
+F32 = mybir.dt.float32
+BF16 = mybir.dt.bfloat16
+U32 = mybir.dt.uint32
+U8 = mybir.dt.uint8
+FP8 = mybir.dt.float8_e4m3fn
+FP8X4 = mybir.dt.float8_e4m3fn_x4
+ALU = mybir.AluOpType
+ACT = mybir.ActivationFunctionType
+AX = mybir.AxisListType
+
+P = 128
+EDGES = 16
+K = 1024
+H = 1024
+HALF = 512
+PASSES = 2
+PACK = 4
+W_CHUNKS = 4
+
+LOAD_EDGES = (2, 1, 1, 2, 2, 4, 4)
+
+W_COPIES = (
+    (("vector", 0, 512),),
+    (("scalar", 0, 512),),
+    (("scalar", 0, 256), ("gpsimd", 256, 512)),
+    (("scalar", 0, 256), ("gpsimd", 256, 512)),
+)
+
+GROUPS = ((0, 1), (1, 2), (2, 3), (3, 4), (4, 6), (6, 8), (8, 11), (11, 14), (14, 16))
+
+SORT_WORDS_FROM = 10
+
+
+def tile_declayerj_pb_kernel(tc, h2_bytes, h2_scale, h_V, mask_attend, W3_w, W3_b, out):
+    nc = tc.nc
+    bytes_view = h2_bytes.rearrange("b n e k -> (b n) e k")
+    scale_view = h2_scale.flatten_outer_dims().rearrange("o (g p t) -> p (o g) t", p=P, t=PACK)
+    mask_view = mask_attend.rearrange("b n e -> (b n) e")
+    residual_view = h_V.rearrange("b n h -> (b n) h")
+    w_view = W3_w.rearrange("(g p j) h -> g p j h", p=P, j=PACK)
+    out_view = out.rearrange("b n h -> (b n) h")
+
+    with ExitStack() as ctx:
+        const = ctx.enter_context(tc.tile_pool(name="const", bufs=1))
+        xb_pool = ctx.enter_context(tc.tile_pool(name="xbp", bufs=6))
+        grp_pool = ctx.enter_context(tc.tile_pool(name="grpp", bufs=4))
+        xp_pool = ctx.enter_context(tc.tile_pool(name="xpp", bufs=6))
+        xt_pool = ctx.enter_context(tc.psum_pool(name="xtp", bufs=6))
+        acc_pool = ctx.enter_context(tc.psum_pool(name="accp", bufs=1))
+        ctx.enter_context(tc.manual_schedule())
+
+        mask_bf = const.tile([P, EDGES], BF16, name="mask_bf")
+        nc.scalar.dma_start(out=mask_bf[:], in_=mask_view)
+        scales = const.tile([P, PASSES, PACK], F32, name="sc")
+        nc.scalar.dma_start(out=scales[:], in_=scale_view)
+
+        byte_tiles = []
+        bytes_of = []
+        for load, n_edges in enumerate(LOAD_EDGES):
+            byte_tile = const.tile([P, n_edges, K], U8, name="h2b%d" % load)
+            byte_tiles.append(byte_tile)
+            bytes_of.extend((byte_tile, slot) for slot in range(n_edges))
+        w_rows = []
+        for chunk in range(W_CHUNKS):
+            w_rows_tile = const.tile([P, PACK, HALF], BF16, name="wraw%d" % chunk)
+            w_rows.append(w_rows_tile)
+
+        def load_bytes(load):
+            first = sum(LOAD_EDGES[:load])
+            nc.sync.dma_start(out=byte_tiles[load][:], in_=bytes_view[:, first : first + LOAD_EDGES[load], :])
+
+        def load_w(chunk):
+            g, half = divmod(chunk, 2)
+            nc.sync.dma_start(out=w_rows[chunk][:], in_=w_view[g][:, :, half * HALF : (half + 1) * HALF])
+
+        for chunk in range(W_CHUNKS):
+            load_bytes(chunk)
+            load_w(chunk)
+        for load in range(W_CHUNKS, len(LOAD_EDGES)):
+            load_bytes(load)
+        residual = const.tile([P, H], BF16, name="hv")
+        nc.sync.dma_start(out=residual[:], in_=residual_view)
+        bias = const.tile([P, H], BF16, name="bias_b")
+        nc.sync.dma_start(out=bias[:], in_=W3_b.partition_broadcast(P))
+
+        ident = const.tile([P, P], F32, name="ident")
+        make_identity(nc, ident[:])
+        zero = const.tile([P, 1], F32, name="zero")
+        nc.vector.memset(zero[:], 0.0)
+        table_warmer = const.tile([P, 1], F32, name="warm")
+        nc.scalar.activation(out=table_warmer[:], in_=zero[:], func=ACT.Copy)
+        mask = const.tile([P, EDGES], F32, name="mask_f")
+        nc.vector.tensor_copy(out=mask[:], in_=mask_bf[:])
+
+        sums = []
+        for half in range(2):
+            sums_tile = acc_pool.tile([P, HALF], F32, name="acc%d" % half)
+            sums.append(sums_tile)
+
+        widened = {}
+        sorted_words = {}
+        turned = {}
+        grouped = {}
+        x_codes = {}
+        x_scales = {}
+        w_grouped = {}
+        w_codes = {}
+        w_scales = {}
+
+        def cast(e):
+            byte_tile, slot = bytes_of[e]
+            fp8_view = byte_tile[:, slot, :].bitcast(FP8)
+            wide = xb_pool.tile([P, K], BF16, name="xb%d" % e, tag="xb")
+            widened[e] = wide
+            if e == 0:
+                nc.vector.tensor_scalar(out=wide[:], in0=fp8_view, scalar1=mask[:, e : e + 1], scalar2=None, op0=ALU.mult)
+            else:
+                nc.scalar.activation(out=wide[:], in_=fp8_view, func=ACT.Copy, scale=mask[:, e : e + 1])
+
+        def sort_words(e):
+            words = xp_pool.tile([P, HALF], F32, name="xp%d" % e, tag="xp")
+            sorted_words[e] = words
+            nc.scalar.copy(
+                out=words[:].rearrange("p (u g w) -> p u g w", u=2, g=2),
+                in_=widened[e][:].bitcast(F32).rearrange("p (g w u) -> p u g w", g=2, u=2),
+            )
+
+        def transposes(e):
+            bank = xt_pool.tile([P, HALF], F32, name="xt%d" % e, tag="xt")
+            turned[e] = bank
+            words = widened[e][:].bitcast(F32)
+            for g in range(PASSES):
+                for u in range(2):
+                    block = slice((2 * u + g) * P, (2 * u + g + 1) * P)
+                    if e in sorted_words:
+                        stationary = sorted_words[e][:, block]
+                    else:
+                        stationary = words[:, 256 * g + u : 256 * (g + 1) : 2]
+                    nc.tensor.transpose(bank[:, block], stationary, ident[:])
+
+        def product(e):
+            tile = grp_pool.tile([P, K], BF16, name="grp%d" % e, tag="grp", align_bytes=256)
+            grouped[e] = tile
+            nc.vector.tensor_tensor(
+                out=tile[:].rearrange("p (g n u i) -> p g n u i", g=2, u=2, i=2),
+                in0=turned[e][:].bitcast(BF16).rearrange("p (u g n i) -> p g n u i", u=2, g=2, i=2),
+                in1=scales[:].rearrange("p g (u i) -> p g u i", u=2).unsqueeze(2).to_broadcast([P, 2, P, 2, 2]),
+                op=ALU.mult,
+            )
+
+        def quantise(e):
+            codes = const.tile([P, PASSES * P], U32, name="xq%d" % e, align_bytes=256)
+            scale_bytes = const.tile([P, PASSES * P], U8, name="xs%d" % e, align_bytes=256)
+            x_codes[e] = codes
+            x_scales[e] = scale_bytes
+            nc.vector.quantize_mx(out=codes[:].bitcast(FP8X4), scales=scale_bytes[:], in_=grouped[e][:])
+
+        def w_interleave(chunk):
+            tile = const.tile([P, HALF, PACK], BF16, name="wgrp%d" % chunk, align_bytes=256)
+            w_grouped[chunk] = tile
+            for engine, first, end in W_COPIES[chunk]:
+                if engine == "gpsimd":
+                    nc.gpsimd.tensor_scalar(
+                        out=tile[:, first:end, :],
+                        in0=w_rows[chunk][:, :, first:end].rearrange("p j c -> p c j"),
+                        scalar1=1.0,
+                        scalar2=0.0,
+                        op0=ALU.mult,
+                        op1=ALU.add,
+                    )
+                else:
+                    dst = tile[:, first:end, :].rearrange("p (c i) j -> p c j i", i=4)
+                    src = w_rows[chunk][:, :, first:end].rearrange("p j (c i) -> p c j i", i=4)
+                    if engine == "vector":
+                        nc.vector.tensor_copy(out=dst, in_=src)
+                    else:
+                        nc.scalar.copy(out=dst, in_=src)
+
+        def w_quantise(chunk):
+            codes = const.tile([P, HALF], U32, name="wq%d" % chunk, align_bytes=256)
+            scale_bytes = const.tile([P, HALF], U8, name="ws%d" % chunk, align_bytes=256)
+            w_codes[chunk] = codes
+            w_scales[chunk] = scale_bytes
+            nc.vector.quantize_mx(
+                out=codes[:].bitcast(FP8X4),
+                scales=scale_bytes[:],
+                in_=w_grouped[chunk][:].rearrange("p c j -> p (c j)"),
+            )
+
+        passes_issued = {0: 0, 1: 0}
+
+        def multiply(e, chunk):
+            g, half = divmod(chunk, 2)
+            nodes = slice(g * P, (g + 1) * P)
+            nc.tensor.matmul_mx(
+                out=sums[half][:],
+                lhsT=x_codes[e][:, nodes].bitcast(FP8X4),
+                lhsT_scale=x_scales[e][:, nodes],
+                rhs=w_codes[chunk][:].bitcast(FP8X4),
+                rhs_scale=w_scales[chunk][:],
+                start=(passes_issued[half] == 0),
+                stop=(passes_issued[half] == EDGES * PASSES - 1),
+            )
+            passes_issued[half] += 1
+
+        multiplied = set()
+        edges_quantised = []
+        chunks_quantised = []
+
+        def multiply_what_is_ready(half_by_half):
+            ready = [(e, chunk) for e in edges_quantised for chunk in chunks_quantised if (e, chunk) not in multiplied]
+            if half_by_half:
+                ready = sorted(ready, key=lambda pair: (pair[1] % 2, pair[0], pair[1]))
+            for e, chunk in ready:
+                multiplied.add((e, chunk))
+                multiply(e, chunk)
+
+        casts_written = set()
+
+        def cast_once(e):
+            if e not in casts_written:
+                casts_written.add(e)
+                cast(e)
+
+        def prepare_group(k):
+            if k < len(GROUPS):
+                members = range(GROUPS[k][0], GROUPS[k][1])
+                for e in members:
+                    cast_once(e)
+                for e in members:
+                    if e >= SORT_WORDS_FROM:
+                        sort_words(e)
+                for e in members:
+                    transposes(e)
+
+        group_ending_at = {}
+        for k, bounds in enumerate(GROUPS):
+            group_ending_at[bounds[1] - 1] = k
+
+        cast_once(0)
+        cast_once(1)
+        for chunk in range(W_CHUNKS):
+            w_interleave(chunk)
+            cast_once(chunk + 2)
+        prepare_group(0)
+        prepare_group(1)
+        for e in range(EDGES):
+            if e <= W_CHUNKS:
+                product(e)
+            if e < W_CHUNKS:
+                w_quantise(e)
+                chunks_quantised.append(e)
+            elif e + 1 < EDGES:
+                product(e + 1)
+            quantise(e)
+            edges_quantised.append(e)
+            if e in group_ending_at:
+                multiply_what_is_ready(e == EDGES - 1)
+                prepare_group(group_ending_at[e] + 2)
+
+        count = const.tile([P, 1], F32, name="cnt")
+        nc.vector.tensor_reduce(out=count[:], in_=mask[:], axis=AX.X, op=ALU.add)
+        count_30th = const.tile([P, 1], F32, name="cnt30")
+        nc.vector.tensor_scalar(out=count_30th[:], in0=count[:], scalar1=1.0 / 30.0, scalar2=None, op0=ALU.mult)
+        rest = const.tile([P, H], F32, name="base")
+        nc.vector.scalar_tensor_tensor(
+            out=rest[:], in0=bias[:], scalar=count_30th[:, 0:1], in1=residual[:], op0=ALU.mult, op1=ALU.add
+        )
+        stores = ((0, 0, 512, nc.sync), (1, 0, 256, nc.sync), (1, 256, 512, nc.scalar))
+        for half, first, end, queue in stores:
+            channels = slice(half * HALF + first, half * HALF + end)
+            result = const.tile([P, end - first], F32, name="res%d_%d" % (half, first))
+            nc.vector.scalar_tensor_tensor(
+                out=result[:], in0=sums[half][:, first:end], scalar=1.0 / 30.0, in1=rest[:, channels], op0=ALU.mult, op1=ALU.add
+            )
+            queue.dma_start(out=out_view[:, channels], in_=result[:])

@@ -35,7 +35,7 @@ W_COPIES = (
 
 GROUPS = ((0, 1), (1, 2), (2, 3), (3, 4), (4, 6), (6, 8), (8, 11), (11, 14), (14, 16))
 
-SORT_WORDS_FROM = 10
+SORT_WORDS_FROM = 4
 
 
 def tile_declayerj_pb_kernel(tc, h2_bytes, h2_scale, h_V, mask_attend, W3_w, W3_b, out):
@@ -99,6 +99,16 @@ def tile_declayerj_pb_kernel(tc, h2_bytes, h2_scale, h_V, mask_attend, W3_w, W3_
         mask = const.tile([P, EDGES], F32, name="mask_f")
         nc.vector.tensor_copy(out=mask[:], in_=mask_bf[:])
 
+        masked_ident = {}
+
+        def mask_identity(e):
+            diag = const.tile([P, P], F32, name="idm%d" % e)
+            masked_ident[e] = diag
+            nc.gpsimd.tensor_scalar(out=diag[:], in0=ident[:], scalar1=mask[:, e : e + 1], scalar2=0.0, op0=ALU.mult, op1=ALU.add)
+
+        for e in range(6):
+            mask_identity(e)
+
         sums = []
         for half in range(2):
             sums_tile = acc_pool.tile([P, HALF], F32, name="acc%d" % half)
@@ -120,9 +130,9 @@ def tile_declayerj_pb_kernel(tc, h2_bytes, h2_scale, h_V, mask_attend, W3_w, W3_
             wide = xb_pool.tile([P, K], BF16, name="xb%d" % e, tag="xb")
             widened[e] = wide
             if e == 0:
-                nc.vector.tensor_scalar(out=wide[:], in0=fp8_view, scalar1=mask[:, e : e + 1], scalar2=None, op0=ALU.mult)
+                nc.vector.tensor_copy(out=wide[:], in_=fp8_view)
             else:
-                nc.scalar.activation(out=wide[:], in_=fp8_view, func=ACT.Copy, scale=mask[:, e : e + 1])
+                nc.scalar.copy(out=wide[:], in_=fp8_view)
 
         def sort_words(e):
             words = xp_pool.tile([P, HALF], F32, name="xp%d" % e, tag="xp")
@@ -143,7 +153,7 @@ def tile_declayerj_pb_kernel(tc, h2_bytes, h2_scale, h_V, mask_attend, W3_w, W3_
                         stationary = sorted_words[e][:, block]
                     else:
                         stationary = words[:, 256 * g + u : 256 * (g + 1) : 2]
-                    nc.tensor.transpose(bank[:, block], stationary, ident[:])
+                    nc.tensor.transpose(bank[:, block], stationary, masked_ident[e][:])
 
         def product(e):
             tile = grp_pool.tile([P, K], BF16, name="grp%d" % e, tag="grp", align_bytes=256)
@@ -249,6 +259,9 @@ def tile_declayerj_pb_kernel(tc, h2_bytes, h2_scale, h_V, mask_attend, W3_w, W3_
         for chunk in range(W_CHUNKS):
             w_interleave(chunk)
             cast_once(chunk + 2)
+            if chunk >= 2:
+                for e in range(5 * chunk - 4, 5 * chunk + 1):
+                    mask_identity(e)
         prepare_group(0)
         prepare_group(1)
         for e in range(EDGES):

@@ -27,11 +27,13 @@ W_CHUNKS = 4
 LOAD_EDGES = (2, 1, 1, 2, 2, 4, 4)
 
 W_COPIES = (
-    (("vector", 0, 512),),
+    (("vector", 0, 256), ("vector", 256, 512)),
     (("scalar", 0, 512),),
     (("scalar", 0, 256), ("gpsimd", 256, 512)),
     (("scalar", 0, 256), ("gpsimd", 256, 512)),
 )
+
+W_LOADS = (((0, 256), (256, 512)), ((0, 512),), ((0, 512),), ((0, 512),))
 
 GROUPS = ((0, 1), (1, 2), (2, 3), (3, 4), (4, 6), (6, 8), (8, 11), (11, 14), (14, 16))
 
@@ -67,10 +69,7 @@ def tile_declayerj_pb_kernel(tc, h2_bytes, h2_scale, h_V, mask_attend, W3_w, W3_
             byte_tile = const.tile([P, n_edges, K], U8, name="h2b%d" % load)
             byte_tiles.append(byte_tile)
             bytes_of.extend((byte_tile, slot) for slot in range(n_edges))
-        w_rows = []
-        for chunk in range(W_CHUNKS):
-            w_rows_tile = const.tile([P, PACK, HALF], BF16, name="wraw%d" % chunk)
-            w_rows.append(w_rows_tile)
+        w_rows = {}
 
         def load_bytes(load):
             first = sum(LOAD_EDGES[:load])
@@ -78,7 +77,11 @@ def tile_declayerj_pb_kernel(tc, h2_bytes, h2_scale, h_V, mask_attend, W3_w, W3_
 
         def load_w(chunk):
             g, half = divmod(chunk, 2)
-            nc.sync.dma_start(out=w_rows[chunk][:], in_=w_view[g][:, :, half * HALF : (half + 1) * HALF])
+            for first, end in W_LOADS[chunk]:
+                rows = const.tile([P, PACK, end - first], BF16, name="wraw%d_%d" % (chunk, first))
+                nc.sync.dma_start(out=rows[:], in_=w_view[g][:, :, half * HALF + first : half * HALF + end])
+                for column in range(first, end, 64):
+                    w_rows[chunk, column] = (rows, first)
 
         for chunk in range(W_CHUNKS):
             load_bytes(chunk)
@@ -179,7 +182,7 @@ def tile_declayerj_pb_kernel(tc, h2_bytes, h2_scale, h_V, mask_attend, W3_w, W3_
                 if engine == "gpsimd":
                     nc.gpsimd.tensor_scalar(
                         out=tile[:, first:end, :],
-                        in0=w_rows[chunk][:, :, first:end].rearrange("p j c -> p c j"),
+                        in0=w_rows[chunk, first][0][:, :, first - w_rows[chunk, first][1] : end - w_rows[chunk, first][1]].rearrange("p j c -> p c j"),
                         scalar1=1.0,
                         scalar2=0.0,
                         op0=ALU.mult,
@@ -187,7 +190,8 @@ def tile_declayerj_pb_kernel(tc, h2_bytes, h2_scale, h_V, mask_attend, W3_w, W3_
                     )
                 else:
                     dst = tile[:, first:end, :].rearrange("p (c i) j -> p c j i", i=4)
-                    src = w_rows[chunk][:, :, first:end].rearrange("p j (c i) -> p c j i", i=4)
+                    rows, start = w_rows[chunk, first]
+                    src = rows[:, :, first - start : end - start].rearrange("p j (c i) -> p c j i", i=4)
                     if engine == "vector":
                         nc.vector.tensor_copy(out=dst, in_=src)
                     else:
@@ -250,6 +254,13 @@ def tile_declayerj_pb_kernel(tc, h2_bytes, h2_scale, h_V, mask_attend, W3_w, W3_
                 for e in members:
                     transposes(e)
 
+        count = const.tile([P, 1], F32, name="cnt")
+        count_30th = const.tile([P, 1], F32, name="cnt30")
+
+        def count_edges():
+            nc.vector.tensor_reduce(out=count[:], in_=mask[:], axis=AX.X, op=ALU.add)
+            nc.vector.tensor_scalar(out=count_30th[:], in0=count[:], scalar1=1.0 / 30.0, scalar2=None, op0=ALU.mult)
+
         group_ending_at = {}
         for k, bounds in enumerate(GROUPS):
             group_ending_at[bounds[1] - 1] = k
@@ -270,18 +281,18 @@ def tile_declayerj_pb_kernel(tc, h2_bytes, h2_scale, h_V, mask_attend, W3_w, W3_
             if e < W_CHUNKS:
                 w_quantise(e)
                 chunks_quantised.append(e)
-            elif e + 1 < EDGES:
+            elif e + 1 < EDGES - 1:
                 product(e + 1)
+            elif e == EDGES - 1:
+                product(e)
+                count_edges()
             quantise(e)
             edges_quantised.append(e)
-            if e in group_ending_at:
+            if e in group_ending_at or e == EDGES - 2:
                 multiply_what_is_ready(e == EDGES - 1)
+            if e in group_ending_at:
                 prepare_group(group_ending_at[e] + 2)
 
-        count = const.tile([P, 1], F32, name="cnt")
-        nc.vector.tensor_reduce(out=count[:], in_=mask[:], axis=AX.X, op=ALU.add)
-        count_30th = const.tile([P, 1], F32, name="cnt30")
-        nc.vector.tensor_scalar(out=count_30th[:], in0=count[:], scalar1=1.0 / 30.0, scalar2=None, op0=ALU.mult)
         rest = const.tile([P, H], F32, name="base")
         nc.vector.scalar_tensor_tensor(
             out=rest[:], in0=bias[:], scalar=count_30th[:, 0:1], in1=residual[:], op0=ALU.mult, op1=ALU.add

@@ -26,18 +26,11 @@ W_CHUNKS = 4
 
 LOAD_EDGES = (2, 1, 1, 2, 2, 4, 4)
 
-W_COPIES = (
-    (("vector", 0, 256), ("vector", 256, 512)),
-    (("scalar", 0, 512),),
-    (("scalar", 0, 256), ("gpsimd", 256, 512)),
-    (("scalar", 0, 256), ("gpsimd", 256, 512)),
-)
-
 W_LOADS = (((0, 256), (256, 512)), ((0, 512),), ((0, 512),), ((0, 512),))
 
 GROUPS = ((0, 1), (1, 2), (2, 3), (3, 4), (4, 6), (6, 8), (8, 11), (11, 14), (14, 16))
 
-SORT_WORDS_FROM = 4
+SORT_WORDS_FROM = 8
 
 
 def tile_declayerj_pb_kernel(tc, h2_bytes, h2_scale, h_V, mask_attend, W3_w, W3_b, out):
@@ -51,7 +44,7 @@ def tile_declayerj_pb_kernel(tc, h2_bytes, h2_scale, h_V, mask_attend, W3_w, W3_
 
     with ExitStack() as ctx:
         const = ctx.enter_context(tc.tile_pool(name="const", bufs=1))
-        xb_pool = ctx.enter_context(tc.tile_pool(name="xbp", bufs=6))
+        xb_pool = ctx.enter_context(tc.tile_pool(name="xbp", bufs=8))
         grp_pool = ctx.enter_context(tc.tile_pool(name="grpp", bufs=4))
         xp_pool = ctx.enter_context(tc.tile_pool(name="xpp", bufs=6))
         xt_pool = ctx.enter_context(tc.psum_pool(name="xtp", bufs=6))
@@ -107,9 +100,9 @@ def tile_declayerj_pb_kernel(tc, h2_bytes, h2_scale, h_V, mask_attend, W3_w, W3_
         def mask_identity(e):
             diag = const.tile([P, P], F32, name="idm%d" % e)
             masked_ident[e] = diag
-            nc.gpsimd.tensor_scalar(out=diag[:], in0=ident[:], scalar1=mask[:, e : e + 1], scalar2=0.0, op0=ALU.mult, op1=ALU.add)
+            nc.vector.tensor_scalar(out=diag[:], in0=ident[:], scalar1=mask[:, e : e + 1], scalar2=None, op0=ALU.mult)
 
-        for e in range(6):
+        for e in range(4):
             mask_identity(e)
 
         sums = []
@@ -117,6 +110,8 @@ def tile_declayerj_pb_kernel(tc, h2_bytes, h2_scale, h_V, mask_attend, W3_w, W3_
             sums_tile = acc_pool.tile([P, HALF], F32, name="acc%d" % half)
             sums.append(sums_tile)
 
+        edges_quantised = []
+        chunks_quantised = []
         widened = {}
         sorted_words = {}
         turned = {}
@@ -127,12 +122,12 @@ def tile_declayerj_pb_kernel(tc, h2_bytes, h2_scale, h_V, mask_attend, W3_w, W3_
         w_codes = {}
         w_scales = {}
 
-        def cast(e):
+        def cast(e, engine="scalar"):
             byte_tile, slot = bytes_of[e]
             fp8_view = byte_tile[:, slot, :].bitcast(FP8)
             wide = xb_pool.tile([P, K], BF16, name="xb%d" % e, tag="xb")
             widened[e] = wide
-            if e == 0:
+            if engine == "vector":
                 nc.vector.tensor_copy(out=wide[:], in_=fp8_view)
             else:
                 nc.scalar.copy(out=wide[:], in_=fp8_view)
@@ -173,35 +168,34 @@ def tile_declayerj_pb_kernel(tc, h2_bytes, h2_scale, h_V, mask_attend, W3_w, W3_
             scale_bytes = const.tile([P, PASSES * P], U8, name="xs%d" % e, align_bytes=256)
             x_codes[e] = codes
             x_scales[e] = scale_bytes
+            edges_quantised.append(e)
             nc.vector.quantize_mx(out=codes[:].bitcast(FP8X4), scales=scale_bytes[:], in_=grouped[e][:])
 
-        def w_interleave(chunk):
-            tile = const.tile([P, HALF, PACK], BF16, name="wgrp%d" % chunk, align_bytes=256)
-            w_grouped[chunk] = tile
-            for engine, first, end in W_COPIES[chunk]:
-                if engine == "gpsimd":
-                    nc.gpsimd.tensor_scalar(
-                        out=tile[:, first:end, :],
-                        in0=w_rows[chunk, first][0][:, :, first - w_rows[chunk, first][1] : end - w_rows[chunk, first][1]].rearrange("p j c -> p c j"),
-                        scalar1=1.0,
-                        scalar2=0.0,
-                        op0=ALU.mult,
-                        op1=ALU.add,
-                    )
-                else:
-                    dst = tile[:, first:end, :].rearrange("p (c i) j -> p c j i", i=4)
-                    rows, start = w_rows[chunk, first]
-                    src = rows[:, :, first - start : end - start].rearrange("p j (c i) -> p c j i", i=4)
-                    if engine == "vector":
-                        nc.vector.tensor_copy(out=dst, in_=src)
-                    else:
-                        nc.scalar.copy(out=dst, in_=src)
+        def w_interleave(chunk, first, end, engine):
+            if chunk not in w_grouped:
+                w_tile = const.tile([P, HALF, PACK], BF16, name="wgrp%d" % chunk, align_bytes=256)
+                w_grouped[chunk] = w_tile
+            rows, start = w_rows[chunk, first]
+            src = rows[:, :, first - start : end - start]
+            dst = w_grouped[chunk][:, first:end, :]
+            if engine == "gpsimd":
+                nc.gpsimd.tensor_scalar(
+                    out=dst, in0=src.rearrange("p j c -> p c j"), scalar1=1.0, scalar2=0.0, op0=ALU.mult, op1=ALU.add
+                )
+                return
+            dst = dst.rearrange("p (c i) j -> p c j i", i=4)
+            src = src.rearrange("p j (c i) -> p c j i", i=4)
+            if engine == "vector":
+                nc.vector.tensor_copy(out=dst, in_=src)
+            else:
+                nc.scalar.copy(out=dst, in_=src)
 
         def w_quantise(chunk):
             codes = const.tile([P, HALF], U32, name="wq%d" % chunk, align_bytes=256)
             scale_bytes = const.tile([P, HALF], U8, name="ws%d" % chunk, align_bytes=256)
             w_codes[chunk] = codes
             w_scales[chunk] = scale_bytes
+            chunks_quantised.append(chunk)
             nc.vector.quantize_mx(
                 out=codes[:].bitcast(FP8X4),
                 scales=scale_bytes[:],
@@ -225,8 +219,6 @@ def tile_declayerj_pb_kernel(tc, h2_bytes, h2_scale, h_V, mask_attend, W3_w, W3_
             passes_issued[half] += 1
 
         multiplied = set()
-        edges_quantised = []
-        chunks_quantised = []
 
         def multiply_what_is_ready(half_by_half):
             ready = [(e, chunk) for e in edges_quantised for chunk in chunks_quantised if (e, chunk) not in multiplied]
@@ -236,18 +228,11 @@ def tile_declayerj_pb_kernel(tc, h2_bytes, h2_scale, h_V, mask_attend, W3_w, W3_
                 multiplied.add((e, chunk))
                 multiply(e, chunk)
 
-        casts_written = set()
-
-        def cast_once(e):
-            if e not in casts_written:
-                casts_written.add(e)
-                cast(e)
-
         def prepare_group(k):
             if k < len(GROUPS):
                 members = range(GROUPS[k][0], GROUPS[k][1])
                 for e in members:
-                    cast_once(e)
+                    cast(e)
                 for e in members:
                     if e >= SORT_WORDS_FROM:
                         sort_words(e)
@@ -265,29 +250,62 @@ def tile_declayerj_pb_kernel(tc, h2_bytes, h2_scale, h_V, mask_attend, W3_w, W3_
         for k, bounds in enumerate(GROUPS):
             group_ending_at[bounds[1] - 1] = k
 
-        cast_once(0)
-        cast_once(1)
-        for chunk in range(W_CHUNKS):
-            w_interleave(chunk)
-            cast_once(chunk + 2)
-            if chunk >= 2:
-                for e in range(5 * chunk - 4, 5 * chunk + 1):
-                    mask_identity(e)
-        prepare_group(0)
-        prepare_group(1)
-        for e in range(EDGES):
-            if e <= W_CHUNKS:
-                product(e)
-            if e < W_CHUNKS:
-                w_quantise(e)
-                chunks_quantised.append(e)
-            elif e + 1 < EDGES - 1:
+        cast(0, "vector")
+        mask_identity(4)
+        cast(1)
+        w_interleave(0, 0, 256, "vector")
+        w_interleave(0, 256, 512, "scalar")
+        cast(2)
+        w_interleave(1, 0, 512, "scalar")
+        cast(3)
+        w_interleave(2, 0, 256, "scalar")
+        w_interleave(2, 256, 512, "gpsimd")
+        cast(4)
+        w_interleave(3, 0, 256, "scalar")
+        cast(5)
+        cast(6)
+        cast(7)
+        transposes(0)
+        transposes(1)
+        product(0)
+        w_quantise(0)
+        quantise(0)
+        multiply_what_is_ready(False)
+        transposes(2)
+        product(1)
+        mask_identity(5)
+        w_quantise(1)
+        quantise(1)
+        multiply_what_is_ready(False)
+        transposes(3)
+        mask_identity(6)
+        transposes(4)
+        product(2)
+        mask_identity(7)
+        w_quantise(2)
+        quantise(2)
+        multiply_what_is_ready(False)
+        transposes(5)
+        w_interleave(3, 256, 512, "vector")
+        product(3)
+        w_quantise(3)
+        quantise(3)
+        transposes(6)
+        multiply_what_is_ready(False)
+        transposes(7)
+        for e in range(4, EDGES):
+            if e == 4:
+                mask_identity(8)
+                mask_identity(9)
+                product(4)
+            if e + 1 < EDGES - 1:
+                if e + 6 < EDGES:
+                    mask_identity(e + 6)
                 product(e + 1)
             elif e == EDGES - 1:
                 product(e)
                 count_edges()
             quantise(e)
-            edges_quantised.append(e)
             if e in group_ending_at or e == EDGES - 2:
                 multiply_what_is_ready(e == EDGES - 1)
             if e in group_ending_at:

@@ -254,17 +254,17 @@ def tile_declayerj_pb_kernel(tc, h2_bytes, h2_scale, h_V, mask_attend, W3_w, W3_
         mask_identity(4)
         cast(1)
         w_interleave(0, 0, 256, "vector")
-        w_interleave(0, 256, 512, "scalar")
+        w_interleave(0, 256, 512, "vector")
         cast(2)
         w_interleave(1, 0, 512, "scalar")
+        w_interleave(2, 0, 512, "scalar")
         cast(3)
-        w_interleave(2, 0, 256, "scalar")
-        w_interleave(2, 256, 512, "gpsimd")
         cast(4)
         w_interleave(3, 0, 256, "scalar")
         cast(5)
         cast(6)
         cast(7)
+        sort_words(7)
         transposes(0)
         transposes(1)
         product(0)

@@ -97,13 +97,16 @@ def tile_declayerj_pb_kernel(tc, h2_bytes, h2_scale, h_V, mask_attend, W3_w, W3_
 
         masked_ident = {}
 
-        def mask_identity(e):
+        def mask_identity(e, engine="scalar"):
             diag = const.tile([P, P], F32, name="idm%d" % e)
             masked_ident[e] = diag
-            nc.vector.tensor_scalar(out=diag[:], in0=ident[:], scalar1=mask[:, e : e + 1], scalar2=None, op0=ALU.mult)
+            if engine == "vector":
+                nc.vector.tensor_scalar(out=diag[:], in0=ident[:], scalar1=mask[:, e : e + 1], scalar2=None, op0=ALU.mult)
+            else:
+                nc.scalar.activation(out=diag[:], in_=ident[:], func=ACT.Copy, scale=mask[:, e : e + 1])
 
-        for e in range(4):
-            mask_identity(e)
+        for e in range(2):
+            mask_identity(e, "vector")
 
         sums = []
         for half in range(2):
@@ -234,6 +237,8 @@ def tile_declayerj_pb_kernel(tc, h2_bytes, h2_scale, h_V, mask_attend, W3_w, W3_
                 for e in members:
                     cast(e)
                 for e in members:
+                    mask_identity(e)
+                for e in members:
                     if e >= SORT_WORDS_FROM:
                         sort_words(e)
                 for e in members:
@@ -251,15 +256,20 @@ def tile_declayerj_pb_kernel(tc, h2_bytes, h2_scale, h_V, mask_attend, W3_w, W3_
             group_ending_at[bounds[1] - 1] = k
 
         cast(0, "vector")
-        mask_identity(4)
         cast(1)
+        mask_identity(2)
+        mask_identity(3)
         w_interleave(0, 0, 256, "vector")
         w_interleave(0, 256, 512, "vector")
         cast(2)
+        mask_identity(4)
+        mask_identity(5)
         w_interleave(1, 0, 512, "scalar")
-        w_interleave(2, 0, 512, "scalar")
+        w_interleave(2, 0, 384, "scalar")
         cast(3)
         cast(4)
+        mask_identity(6)
+        mask_identity(7)
         w_interleave(3, 0, 256, "scalar")
         cast(5)
         cast(6)
@@ -273,15 +283,13 @@ def tile_declayerj_pb_kernel(tc, h2_bytes, h2_scale, h_V, mask_attend, W3_w, W3_
         multiply_what_is_ready(False)
         transposes(2)
         product(1)
-        mask_identity(5)
         w_quantise(1)
         quantise(1)
         multiply_what_is_ready(False)
         transposes(3)
-        mask_identity(6)
         transposes(4)
+        w_interleave(2, 384, 512, "vector")
         product(2)
-        mask_identity(7)
         w_quantise(2)
         quantise(2)
         multiply_what_is_ready(False)
@@ -295,12 +303,8 @@ def tile_declayerj_pb_kernel(tc, h2_bytes, h2_scale, h_V, mask_attend, W3_w, W3_
         transposes(7)
         for e in range(4, EDGES):
             if e == 4:
-                mask_identity(8)
-                mask_identity(9)
                 product(4)
             if e + 1 < EDGES - 1:
-                if e + 6 < EDGES:
-                    mask_identity(e + 6)
                 product(e + 1)
             elif e == EDGES - 1:
                 product(e)

@@ -24,13 +24,12 @@ PASSES = 2
 PACK = 4
 W_CHUNKS = 4
 
-LOAD_EDGES = (2, 1, 1, 2, 2, 4, 4)
+LOAD_EDGES = (2, 2, 2, 2, 4, 4)
 
 W_LOADS = (((0, 256), (256, 512)), ((0, 512),), ((0, 512),), ((0, 512),))
 
-GROUPS = ((0, 1), (1, 2), (2, 3), (3, 4), (4, 6), (6, 8), (8, 11), (11, 14), (14, 16))
-
-SORT_WORDS_FROM = 8
+RUN_FROM = 8
+RUN = 3
 
 
 def tile_declayerj_pb_kernel(tc, h2_bytes, h2_scale, h_V, mask_attend, W3_w, W3_b, out):
@@ -90,10 +89,10 @@ def tile_declayerj_pb_kernel(tc, h2_bytes, h2_scale, h_V, mask_attend, W3_w, W3_
         make_identity(nc, ident[:])
         zero = const.tile([P, 1], F32, name="zero")
         nc.vector.memset(zero[:], 0.0)
+        zeros = const.tile([P, HALF], BF16, name="zeros")
+        nc.vector.memset(zeros[:], 0.0)
         table_warmer = const.tile([P, 1], F32, name="warm")
         nc.scalar.activation(out=table_warmer[:], in_=zero[:], func=ACT.Copy)
-        mask = const.tile([P, EDGES], F32, name="mask_f")
-        nc.vector.tensor_copy(out=mask[:], in_=mask_bf[:])
 
         masked_ident = {}
 
@@ -101,17 +100,23 @@ def tile_declayerj_pb_kernel(tc, h2_bytes, h2_scale, h_V, mask_attend, W3_w, W3_
             diag = const.tile([P, P], F32, name="idm%d" % e)
             masked_ident[e] = diag
             if engine == "vector":
-                nc.vector.tensor_scalar(out=diag[:], in0=ident[:], scalar1=mask[:, e : e + 1], scalar2=None, op0=ALU.mult)
+                nc.vector.tensor_scalar(out=diag[:], in0=ident[:], scalar1=mask_bf[:, e : e + 1], scalar2=None, op0=ALU.mult)
             else:
                 nc.scalar.activation(out=diag[:], in_=ident[:], func=ACT.Copy, scale=mask[:, e : e + 1])
 
-        for e in range(2):
+        for e in range(4):
             mask_identity(e, "vector")
+        mask = const.tile([P, EDGES], F32, name="mask_f")
+        nc.vector.tensor_copy(out=mask[:], in_=mask_bf[:])
 
         sums = []
         for half in range(2):
             sums_tile = acc_pool.tile([P, HALF], F32, name="acc%d" % half)
             sums.append(sums_tile)
+
+        def dummy_matmuls(n):
+            for i in range(n):
+                nc.tensor.matmul(sums[1][:], lhsT=zeros[:, 0:P], rhs=zeros[:], start=True, stop=True)
 
         edges_quantised = []
         chunks_quantised = []
@@ -231,18 +236,15 @@ def tile_declayerj_pb_kernel(tc, h2_bytes, h2_scale, h_V, mask_attend, W3_w, W3_
                 multiplied.add((e, chunk))
                 multiply(e, chunk)
 
-        def prepare_group(k):
-            if k < len(GROUPS):
-                members = range(GROUPS[k][0], GROUPS[k][1])
-                for e in members:
-                    cast(e)
-                for e in members:
-                    mask_identity(e)
-                for e in members:
-                    if e >= SORT_WORDS_FROM:
-                        sort_words(e)
-                for e in members:
-                    transposes(e)
+        def multiply_edge(e):
+            for chunk in chunks_quantised:
+                multiplied.add((e, chunk))
+                multiply(e, chunk)
+
+        def prepare(e):
+            cast(e)
+            mask_identity(e)
+            sort_words(e)
 
         count = const.tile([P, 1], F32, name="cnt")
         count_30th = const.tile([P, 1], F32, name="cnt30")
@@ -251,69 +253,76 @@ def tile_declayerj_pb_kernel(tc, h2_bytes, h2_scale, h_V, mask_attend, W3_w, W3_
             nc.vector.tensor_reduce(out=count[:], in_=mask[:], axis=AX.X, op=ALU.add)
             nc.vector.tensor_scalar(out=count_30th[:], in0=count[:], scalar1=1.0 / 30.0, scalar2=None, op0=ALU.mult)
 
-        group_ending_at = {}
-        for k, bounds in enumerate(GROUPS):
-            group_ending_at[bounds[1] - 1] = k
-
         cast(0, "vector")
         cast(1)
-        mask_identity(2)
-        mask_identity(3)
+        for e in range(4, 8):
+            mask_identity(e)
         w_interleave(0, 0, 256, "vector")
         w_interleave(0, 256, 512, "vector")
         cast(2)
-        mask_identity(4)
-        mask_identity(5)
-        w_interleave(1, 0, 512, "scalar")
-        w_interleave(2, 0, 384, "scalar")
         cast(3)
+        w_interleave(1, 0, 512, "scalar")
+        w_interleave(2, 0, 512, "scalar")
         cast(4)
-        mask_identity(6)
-        mask_identity(7)
-        w_interleave(3, 0, 256, "scalar")
         cast(5)
+        w_interleave(3, 0, 256, "scalar")
         cast(6)
         cast(7)
         sort_words(7)
+        dummy_matmuls(8)
         transposes(0)
         transposes(1)
+        dummy_matmuls(1)
+        transposes(2)
+        dummy_matmuls(1)
         product(0)
         w_quantise(0)
         quantise(0)
         multiply_what_is_ready(False)
-        transposes(2)
+        dummy_matmuls(1)
         product(1)
         w_quantise(1)
         quantise(1)
         multiply_what_is_ready(False)
         transposes(3)
         transposes(4)
-        w_interleave(2, 384, 512, "vector")
         product(2)
         w_quantise(2)
         quantise(2)
         multiply_what_is_ready(False)
         transposes(5)
+        transposes(6)
         w_interleave(3, 256, 512, "vector")
         product(3)
         w_quantise(3)
         quantise(3)
-        transposes(6)
         multiply_what_is_ready(False)
         transposes(7)
-        for e in range(4, EDGES):
-            if e == 4:
-                product(4)
-            if e + 1 < EDGES - 1:
-                product(e + 1)
-            elif e == EDGES - 1:
-                product(e)
-                count_edges()
-            quantise(e)
-            if e in group_ending_at or e == EDGES - 2:
-                multiply_what_is_ready(e == EDGES - 1)
-            if e in group_ending_at:
-                prepare_group(group_ending_at[e] + 2)
+        product(4)
+        product(5)
+        quantise(4)
+        multiply_what_is_ready(False)
+        product(6)
+        quantise(5)
+        product(7)
+        quantise(6)
+        for e in range(RUN_FROM, EDGES - 1):
+            if (e - RUN_FROM) % RUN == 0:
+                run = range(e, min(e + RUN, EDGES))
+                for turned_edge in run:
+                    prepare(turned_edge)
+                for turned_edge in run:
+                    transposes(turned_edge)
+            product(e)
+            quantise(e - 1)
+            multiply_edge(e - RUN)
+        quantise(EDGES - 2)
+        for e in range(EDGES - 1 - RUN, EDGES - 1):
+            multiply_edge(e)
+        product(EDGES - 1)
+        count_edges()
+        quantise(EDGES - 1)
+        multiply_what_is_ready(True)
 
         rest = const.tile([P, H], F32, name="base")
         nc.vector.scalar_tensor_tensor(

@@ -89,8 +89,6 @@ def tile_declayerj_pb_kernel(tc, h2_bytes, h2_scale, h_V, mask_attend, W3_w, W3_
         make_identity(nc, ident[:])
         zero = const.tile([P, 1], F32, name="zero")
         nc.vector.memset(zero[:], 0.0)
-        zeros = const.tile([P, HALF], BF16, name="zeros")
-        nc.vector.memset(zeros[:], 0.0)
         table_warmer = const.tile([P, 1], F32, name="warm")
         nc.scalar.activation(out=table_warmer[:], in_=zero[:], func=ACT.Copy)
 
@@ -113,10 +111,6 @@ def tile_declayerj_pb_kernel(tc, h2_bytes, h2_scale, h_V, mask_attend, W3_w, W3_
         for half in range(2):
             sums_tile = acc_pool.tile([P, HALF], F32, name="acc%d" % half)
             sums.append(sums_tile)
-
-        def dummy_matmuls(n):
-            for i in range(n):
-                nc.tensor.matmul(sums[1][:], lhsT=zeros[:, 0:P], rhs=zeros[:], start=True, stop=True)
 
         edges_quantised = []
         chunks_quantised = []
@@ -261,43 +255,39 @@ def tile_declayerj_pb_kernel(tc, h2_bytes, h2_scale, h_V, mask_attend, W3_w, W3_
         w_interleave(0, 256, 512, "vector")
         cast(2)
         cast(3)
-        w_interleave(1, 0, 512, "scalar")
-        w_interleave(2, 0, 512, "scalar")
+        w_interleave(1, 0, 256, "scalar")
         cast(4)
         cast(5)
+        w_interleave(2, 0, 384, "scalar")
+        w_interleave(2, 384, 512, "gpsimd")
         w_interleave(3, 0, 256, "scalar")
         cast(6)
         cast(7)
         sort_words(7)
-        dummy_matmuls(8)
-        transposes(0)
-        transposes(1)
-        dummy_matmuls(1)
-        transposes(2)
-        dummy_matmuls(1)
+        for e in range(4):
+            transposes(e)
         product(0)
         w_quantise(0)
         quantise(0)
         multiply_what_is_ready(False)
-        dummy_matmuls(1)
+        w_interleave(1, 256, 512, "vector")
         product(1)
         w_quantise(1)
         quantise(1)
         multiply_what_is_ready(False)
-        transposes(3)
         transposes(4)
+        transposes(5)
         product(2)
         w_quantise(2)
         quantise(2)
         multiply_what_is_ready(False)
-        transposes(5)
         transposes(6)
+        transposes(7)
         w_interleave(3, 256, 512, "vector")
         product(3)
         w_quantise(3)
         quantise(3)
         multiply_what_is_ready(False)
-        transposes(7)
         product(4)
         product(5)
         quantise(4)

@@ -53,7 +53,6 @@ def tile_declayerj_pb_kernel(tc, h2_bytes, h2_scale, h_V, mask_attend, W3_w, W3_
         mask_bf = const.tile([P, EDGES], BF16, name="mask_bf")
         nc.scalar.dma_start(out=mask_bf[:], in_=mask_view)
         scales = const.tile([P, PASSES, PACK], F32, name="sc")
-        nc.scalar.dma_start(out=scales[:], in_=scale_view)
 
         byte_tiles = []
         bytes_of = []
@@ -91,6 +90,7 @@ def tile_declayerj_pb_kernel(tc, h2_bytes, h2_scale, h_V, mask_attend, W3_w, W3_
         nc.vector.memset(zero[:], 0.0)
         table_warmer = const.tile([P, 1], F32, name="warm")
         nc.scalar.activation(out=table_warmer[:], in_=zero[:], func=ACT.Copy)
+        nc.scalar.dma_start(out=scales[:], in_=scale_view)
 
         masked_ident = {}
 

@@ -252,7 +252,7 @@ def tile_declayerj_pb_kernel(tc, h2_bytes, h2_scale, h_V, mask_attend, W3_w, W3_
         for e in range(4, 8):
             mask_identity(e)
         w_interleave(0, 0, 256, "vector")
-        w_interleave(0, 256, 512, "vector")
+        w_interleave(0, 256, 512, "scalar")
         cast(2)
         cast(3)
         w_interleave(1, 0, 256, "scalar")
@@ -260,6 +260,7 @@ def tile_declayerj_pb_kernel(tc, h2_bytes, h2_scale, h_V, mask_attend, W3_w, W3_
         cast(5)
         w_interleave(2, 0, 384, "scalar")
         w_interleave(2, 384, 512, "gpsimd")
+        w_interleave(3, 256, 384, "gpsimd")
         w_interleave(3, 0, 256, "scalar")
         cast(6)
         cast(7)
@@ -283,7 +284,7 @@ def tile_declayerj_pb_kernel(tc, h2_bytes, h2_scale, h_V, mask_attend, W3_w, W3_
         multiply_what_is_ready(False)
         transposes(6)
         transposes(7)
-        w_interleave(3, 256, 512, "vector")
+        w_interleave(3, 384, 512, "vector")
         product(3)
         w_quantise(3)
         quantise(3)

from contextlib import ExitStack

import concourse.mybir as mybir
from concourse.masks import make_identity

FLOPS = 2 * 2048 * 1024 * 1024

F32 = mybir.dt.float32
BF16 = mybir.dt.bfloat16
U32 = mybir.dt.uint32
U8 = mybir.dt.uint8
FP8 = mybir.dt.float8_e4m3fn
FP8X4 = mybir.dt.float8_e4m3fn_x4
ALU = mybir.AluOpType
ACT = mybir.ActivationFunctionType
AX = mybir.AxisListType

P = 128
EDGES = 16
K = 1024
H = 1024
HALF = 512
PASSES = 2
PACK = 4
W_CHUNKS = 4

LOAD_EDGES = (2, 2, 2, 2, 4, 4)

W_LOADS = (((0, 256), (256, 512)), ((0, 512),), ((0, 512),), ((0, 512),))

RUN_FROM = 8
RUN = 3


def tile_declayerj_pb_kernel(tc, h2_bytes, h2_scale, h_V, mask_attend, W3_w, W3_b, out):
    nc = tc.nc
    bytes_view = h2_bytes.rearrange("b n e k -> (b n) e k")
    scale_view = h2_scale.flatten_outer_dims().rearrange("o (g p t) -> p (o g) t", p=P, t=PACK)
    mask_view = mask_attend.rearrange("b n e -> (b n) e")
    residual_view = h_V.rearrange("b n h -> (b n) h")
    w_view = W3_w.rearrange("(g p j) h -> g p j h", p=P, j=PACK)
    out_view = out.rearrange("b n h -> (b n) h")

    with ExitStack() as ctx:
        const = ctx.enter_context(tc.tile_pool(name="const", bufs=1))
        xb_pool = ctx.enter_context(tc.tile_pool(name="xbp", bufs=8))
        grp_pool = ctx.enter_context(tc.tile_pool(name="grpp", bufs=4))
        xp_pool = ctx.enter_context(tc.tile_pool(name="xpp", bufs=6))
        xt_pool = ctx.enter_context(tc.psum_pool(name="xtp", bufs=6))
        acc_pool = ctx.enter_context(tc.psum_pool(name="accp", bufs=1))
        ctx.enter_context(tc.manual_schedule())

        mask_bf = const.tile([P, EDGES], BF16, name="mask_bf")
        nc.scalar.dma_start(out=mask_bf[:], in_=mask_view)
        scales = const.tile([P, PASSES, PACK], F32, name="sc")

        byte_tiles = []
        bytes_of = []
        for load, n_edges in enumerate(LOAD_EDGES):
            byte_tile = const.tile([P, n_edges, K], U8, name="h2b%d" % load)
            byte_tiles.append(byte_tile)
            bytes_of.extend((byte_tile, slot) for slot in range(n_edges))
        w_rows = {}

        def load_bytes(load):
            first = sum(LOAD_EDGES[:load])
            nc.sync.dma_start(out=byte_tiles[load][:], in_=bytes_view[:, first : first + LOAD_EDGES[load], :])

        def load_w(chunk):
            g, half = divmod(chunk, 2)
            for first, end in W_LOADS[chunk]:
                rows = const.tile([P, PACK, end - first], BF16, name="wraw%d_%d" % (chunk, first))
                nc.sync.dma_start(out=rows[:], in_=w_view[g][:, :, half * HALF + first : half * HALF + end])
                for column in range(first, end, 64):
                    w_rows[chunk, column] = (rows, first)

        for chunk in range(W_CHUNKS):
            load_bytes(chunk)
            load_w(chunk)
        for load in range(W_CHUNKS, len(LOAD_EDGES)):
            load_bytes(load)
        residual = const.tile([P, H], BF16, name="hv")
        nc.sync.dma_start(out=residual[:], in_=residual_view)
        bias = const.tile([P, H], BF16, name="bias_b")
        nc.sync.dma_start(out=bias[:], in_=W3_b.partition_broadcast(P))

        ident = const.tile([P, P], F32, name="ident")
        make_identity(nc, ident[:])
        zero = const.tile([P, 1], F32, name="zero")
        nc.vector.memset(zero[:], 0.0)
        table_warmer = const.tile([P, 1], F32, name="warm")
        nc.scalar.activation(out=table_warmer[:], in_=zero[:], func=ACT.Copy)
        nc.scalar.dma_start(out=scales[:], in_=scale_view)

        masked_ident = {}

        def mask_identity(e, engine="scalar"):
            diag = const.tile([P, P], F32, name="idm%d" % e)
            masked_ident[e] = diag
            if engine == "vector":
                nc.vector.tensor_scalar(out=diag[:], in0=ident[:], scalar1=mask_bf[:, e : e + 1], scalar2=None, op0=ALU.mult)
            else:
                nc.scalar.activation(out=diag[:], in_=ident[:], func=ACT.Copy, scale=mask[:, e : e + 1])

        for e in range(4):
            mask_identity(e, "vector")
        mask = const.tile([P, EDGES], F32, name="mask_f")
        nc.vector.tensor_copy(out=mask[:], in_=mask_bf[:])

        sums = []
        for half in range(2):
            sums_tile = acc_pool.tile([P, HALF], F32, name="acc%d" % half)
            sums.append(sums_tile)

        edges_quantised = []
        chunks_quantised = []
        widened = {}
        sorted_words = {}
        turned = {}
        grouped = {}
        x_codes = {}
        x_scales = {}
        w_grouped = {}
        w_codes = {}
        w_scales = {}

        def cast(e, engine="scalar"):
            byte_tile, slot = bytes_of[e]
            fp8_view = byte_tile[:, slot, :].bitcast(FP8)
            wide = xb_pool.tile([P, K], BF16, name="xb%d" % e, tag="xb")
            widened[e] = wide
            if engine == "vector":
                nc.vector.tensor_copy(out=wide[:], in_=fp8_view)
            else:
                nc.scalar.copy(out=wide[:], in_=fp8_view)

        def sort_words(e):
            words = xp_pool.tile([P, HALF], F32, name="xp%d" % e, tag="xp")
            sorted_words[e] = words
            nc.scalar.copy(
                out=words[:].rearrange("p (u g w) -> p u g w", u=2, g=2),
                in_=widened[e][:].bitcast(F32).rearrange("p (g w u) -> p u g w", g=2, u=2),
            )

        def transposes(e):
            bank = xt_pool.tile([P, HALF], F32, name="xt%d" % e, tag="xt")
            turned[e] = bank
            words = widened[e][:].bitcast(F32)
            for g in range(PASSES):
                for u in range(2):
                    block = slice((2 * u + g) * P, (2 * u + g + 1) * P)
                    if e in sorted_words:
                        stationary = sorted_words[e][:, block]
                    else:
                        stationary = words[:, 256 * g + u : 256 * (g + 1) : 2]
                    nc.tensor.transpose(bank[:, block], stationary, masked_ident[e][:])

        def product(e):
            tile = grp_pool.tile([P, K], BF16, name="grp%d" % e, tag="grp", align_bytes=256)
            grouped[e] = tile
            nc.vector.tensor_tensor(
                out=tile[:].rearrange("p (g n u i) -> p g n u i", g=2, u=2, i=2),
                in0=turned[e][:].bitcast(BF16).rearrange("p (u g n i) -> p g n u i", u=2, g=2, i=2),
                in1=scales[:].rearrange("p g (u i) -> p g u i", u=2).unsqueeze(2).to_broadcast([P, 2, P, 2, 2]),
                op=ALU.mult,
            )

        def quantise(e):
            codes = const.tile([P, PASSES * P], U32, name="xq%d" % e, align_bytes=256)
            scale_bytes = const.tile([P, PASSES * P], U8, name="xs%d" % e, align_bytes=256)
            x_codes[e] = codes
            x_scales[e] = scale_bytes
            edges_quantised.append(e)
            nc.vector.quantize_mx(out=codes[:].bitcast(FP8X4), scales=scale_bytes[:], in_=grouped[e][:])

        def w_interleave(chunk, first, end, engine):
            if chunk not in w_grouped:
                w_tile = const.tile([P, HALF, PACK], BF16, name="wgrp%d" % chunk, align_bytes=256)
                w_grouped[chunk] = w_tile
            rows, start = w_rows[chunk, first]
            src = rows[:, :, first - start : end - start]
            dst = w_grouped[chunk][:, first:end, :]
            if engine == "gpsimd":
                nc.gpsimd.tensor_scalar(
                    out=dst, in0=src.rearrange("p j c -> p c j"), scalar1=1.0, scalar2=0.0, op0=ALU.mult, op1=ALU.add
                )
                return
            dst = dst.rearrange("p (c i) j -> p c j i", i=4)
            src = src.rearrange("p j (c i) -> p c j i", i=4)
            if engine == "vector":
                nc.vector.tensor_copy(out=dst, in_=src)
            else:
                nc.scalar.copy(out=dst, in_=src)

        def w_quantise(chunk):
            codes = const.tile([P, HALF], U32, name="wq%d" % chunk, align_bytes=256)
            scale_bytes = const.tile([P, HALF], U8, name="ws%d" % chunk, align_bytes=256)
            w_codes[chunk] = codes
            w_scales[chunk] = scale_bytes
            chunks_quantised.append(chunk)
            nc.vector.quantize_mx(
                out=codes[:].bitcast(FP8X4),
                scales=scale_bytes[:],
                in_=w_grouped[chunk][:].rearrange("p c j -> p (c j)"),
            )

        passes_issued = {0: 0, 1: 0}

        def multiply(e, chunk):
            g, half = divmod(chunk, 2)
            nodes = slice(g * P, (g + 1) * P)
            nc.tensor.matmul_mx(
                out=sums[half][:],
                lhsT=x_codes[e][:, nodes].bitcast(FP8X4),
                lhsT_scale=x_scales[e][:, nodes],
                rhs=w_codes[chunk][:].bitcast(FP8X4),
                rhs_scale=w_scales[chunk][:],
                start=(passes_issued[half] == 0),
                stop=(passes_issued[half] == EDGES * PASSES - 1),
            )
            passes_issued[half] += 1

        multiplied = set()

        def multiply_what_is_ready(half_by_half):
            ready = [(e, chunk) for e in edges_quantised for chunk in chunks_quantised if (e, chunk) not in multiplied]
            if half_by_half:
                ready = sorted(ready, key=lambda pair: (pair[1] % 2, pair[0], pair[1]))
            for e, chunk in ready:
                multiplied.add((e, chunk))
                multiply(e, chunk)

        def multiply_edge(e):
            for chunk in chunks_quantised:
                multiplied.add((e, chunk))
                multiply(e, chunk)

        def prepare(e):
            cast(e)
            mask_identity(e)
            sort_words(e)

        count = const.tile([P, 1], F32, name="cnt")
        count_30th = const.tile([P, 1], F32, name="cnt30")

        def count_edges():
            nc.vector.tensor_reduce(out=count[:], in_=mask[:], axis=AX.X, op=ALU.add)
            nc.vector.tensor_scalar(out=count_30th[:], in0=count[:], scalar1=1.0 / 30.0, scalar2=None, op0=ALU.mult)

        cast(0, "vector")
        cast(1)
        for e in range(4, 8):
            mask_identity(e)
        w_interleave(0, 0, 256, "vector")
        w_interleave(0, 256, 512, "scalar")
        cast(2)
        cast(3)
        w_interleave(1, 0, 256, "scalar")
        cast(4)
        cast(5)
        w_interleave(2, 0, 384, "scalar")
        w_interleave(2, 384, 512, "gpsimd")
        w_interleave(3, 256, 384, "gpsimd")
        w_interleave(3, 0, 256, "scalar")
        cast(6)
        cast(7)
        sort_words(7)
        for e in range(4):
            transposes(e)
        product(0)
        w_quantise(0)
        quantise(0)
        multiply_what_is_ready(False)
        w_interleave(1, 256, 512, "vector")
        product(1)
        w_quantise(1)
        quantise(1)
        multiply_what_is_ready(False)
        transposes(4)
        transposes(5)
        product(2)
        w_quantise(2)
        quantise(2)
        multiply_what_is_ready(False)
        transposes(6)
        transposes(7)
        w_interleave(3, 384, 512, "vector")
        product(3)
        w_quantise(3)
        quantise(3)
        multiply_what_is_ready(False)
        product(4)
        product(5)
        quantise(4)
        multiply_what_is_ready(False)
        product(6)
        quantise(5)
        product(7)
        quantise(6)
        for e in range(RUN_FROM, EDGES - 1):
            if (e - RUN_FROM) % RUN == 0:
                run = range(e, min(e + RUN, EDGES))
                for turned_edge in run:
                    prepare(turned_edge)
                for turned_edge in run:
                    transposes(turned_edge)
            product(e)
            quantise(e - 1)
            multiply_edge(e - RUN)
        quantise(EDGES - 2)
        for e in range(EDGES - 1 - RUN, EDGES - 1):
            multiply_edge(e)
        product(EDGES - 1)
        count_edges()
        quantise(EDGES - 1)
        multiply_what_is_ready(True)

        rest = const.tile([P, H], F32, name="base")
        nc.vector.scalar_tensor_tensor(
            out=rest[:], in0=bias[:], scalar=count_30th[:, 0:1], in1=residual[:], op0=ALU.mult, op1=ALU.add
        )
        stores = ((0, 0, 512, nc.sync), (1, 0, 256, nc.sync), (1, 256, 512, nc.scalar))
        for half, first, end, queue in stores:
            channels = slice(half * HALF + first, half * HALF + end)
            result = const.tile([P, end - first], F32, name="res%d_%d" % (half, first))
            nc.vector.scalar_tensor_tensor(
                out=result[:], in0=sums[half][:, first:end], scalar=1.0 / 30.0, in1=rest[:, channels], op0=ALU.mult, op1=ALU.add
            )
            queue.dma_start(out=out_view[:, channels], in_=result[:])
